import numpy as np
import ml_dtypes


def mxq(x, axis, fmt="e4m3"):
    dtype, down = {"e4m3": (ml_dtypes.float8_e4m3fn, 7), "e5m2": (ml_dtypes.float8_e5m2, 14)}[fmt]
    v = np.moveaxis(np.asarray(x, np.float32).astype(ml_dtypes.bfloat16).astype(np.float64), axis, -1)
    blocks = v.reshape(v.shape[:-1] + (-1, 32))
    amax = np.abs(blocks).max(-1, keepdims=True)
    byte = np.maximum(np.where(amax > 0, np.frexp(amax)[1] - 1 + 127, 0) - down, 1)
    scale = np.exp2(byte - 127.0)
    codes = (blocks / scale).astype(np.float32).astype(dtype).astype(np.float64)
    return np.moveaxis((codes * scale).reshape(v.shape), -1, axis)


WIDE = False


def mx_kscale(k):
    if not WIDE:
        return np.ones(k)
    levels = np.array([10, -10, 5, -5, 0])
    a = np.random.permutation(np.resize(levels, k // 512 * 4)).reshape(k // 512, 4)
    idx = np.arange(k)
    return np.exp2(a[idx // 512, idx % 128 // 32])


BF16 = ml_dtypes.bfloat16


def bf(x):
    return np.asarray(x, np.float32).astype(BF16)


def f64(x):
    return np.asarray(x).astype(np.float64)


NB, S, DI, DO, R = 4, 128, 2048, 2048, 512
SCALE = 0.125


def setup_inputs():
    s, t = mx_kscale(R), mx_kscale(DI)
    return {"x": bf(np.random.standard_normal((NB, S, DI)) * t),
            "A": bf(np.random.standard_normal((R, DI)) * 3.0 / np.sqrt(DI) / s[:, None] / t),
            "B": bf(np.random.standard_normal((DO, R)) * 3.0 / np.sqrt(R) * s),
            "d_A": bf(1.0 + 0.1 * np.random.standard_normal(R)),
            "d_B": bf(np.random.standard_normal(DO))}


def reference(x, A, B, d_A, d_B):
    scaled_A = f64(d_A)[:, None] * f64(A)
    BA = mxq(f64(B), 1, "e4m3") @ mxq(scaled_A, 0, "e4m3")
    W = f64(d_B)[:, None] * BA
    return (mxq(f64(x), 2, "e4m3") @ mxq(W, 1, "e4m3").T) * SCALE

@@ -1,0 +1,233 @@
+from contextlib import ExitStack
+
+import concourse.mybir as mybir
+from concourse.masks import make_identity
+
+F32 = mybir.dt.float32
+BF16 = mybir.dt.bfloat16
+U32 = mybir.dt.uint32
+U8 = mybir.dt.uint8
+FP8X4 = mybir.dt.float8_e4m3fn_x4
+MULT = mybir.AluOpType.mult
+COPY = mybir.ActivationFunctionType.Copy
+
+P = 128
+TOK, DI, DO, R = 512, 2048, 2048, 512
+CH = 512
+NG = DI // CH
+NOC = DO // CH
+SCALE = 0.125
+FLOPS = 2 * DO * DI * R + 2 * TOK * DI * DO
+
+
+def tile_veralayer_pa_kernel(tc, x, A, B, d_A, d_B, out):
+    nc = tc.nc
+    with ExitStack() as ctx:
+        const = ctx.enter_context(tc.tile_pool(name="const", bufs=1))
+        raw = ctx.enter_context(tc.tile_pool(name="raw", bufs=1))
+        keep = ctx.enter_context(tc.tile_pool(name="keep", bufs=1))
+        grp = ctx.enter_context(tc.tile_pool(name="grp", bufs=3))
+        wgp = ctx.enter_context(tc.tile_pool(name="wgp", bufs=3))
+        wcp = ctx.enter_context(tc.tile_pool(name="wcp", bufs=3))
+        outp = ctx.enter_context(tc.tile_pool(name="outp", bufs=4))
+        ps_wk = ctx.enter_context(tc.psum_pool(name="ps_wk", bufs=4))
+        ps_acc = ctx.enter_context(tc.psum_pool(name="ps_acc", bufs=1))
+
+        x_v = x.rearrange("b s i -> (b s) i").rearrange("(tt p) i -> p tt i", p=P)
+        out_v = out.rearrange("b s o -> (b s) o")
+        a_v = A.rearrange("(u p e) i -> u p e i", u=2, e=2)
+        b_v = B.rearrange("(ot p) r -> p ot r", p=P)
+
+        zrow = const.tile([P, DO], BF16)
+        ones = const.tile([P, P], BF16)
+        ident_f = const.tile([P, P], F32)
+        ident_b = const.tile([P, P], BF16)
+        da_b = const.tile([P, 4], BF16)
+        da_f = const.tile([P, 4], F32)
+        diag = const.tile([P, 4, P], BF16)
+        db_bc = const.tile([P, DO], BF16)
+
+        nc.scalar.dma_start(
+            out=da_b[:].rearrange("p (u e) -> p u e", u=2),
+            in_=d_A.rearrange("(u p e) -> p u e", u=2, e=2),
+        )
+        nc.vector.memset(zrow[:], 0.0)
+        nc.scalar.dma_start(out=zrow[0:1, :], in_=d_B.rearrange("(a n) -> a n", a=1))
+        nc.vector.memset(ones[:], 1.0)
+        make_identity(nc, ident_b[:])
+        make_identity(nc, ident_f[:])
+
+        a_raw = [raw.tile([P, 4, CH], BF16, name="a_raw%d" % g) for g in range(NG)]
+        x_raw = [raw.tile([P, 4 * CH], BF16, name="x_raw%d" % g) for g in range(NG)]
+        b_raw = [raw.tile([P, 4 * R], BF16, name="b_raw%d" % c) for c in range(NOC)]
+
+        def load_a(g):
+            for u in range(2):
+                nc.sync.dma_start(
+                    out=a_raw[g][:, 2 * u : 2 * u + 2, :],
+                    in_=a_v[u][:, :, g * CH : (g + 1) * CH],
+                )
+
+        def load_x(g):
+            nc.sync.dma_start(
+                out=x_raw[g][:].rearrange("p (tt i) -> p tt i", tt=4),
+                in_=x_v[:, :, g * CH : (g + 1) * CH],
+            )
+
+        def load_b(c):
+            nc.sync.dma_start(
+                out=b_raw[c][:].rearrange("p (ot r) -> p ot r", ot=4),
+                in_=b_v[:, 4 * c : 4 * c + 4, :],
+            )
+
+        load_a(0)
+        load_b(0)
+        load_a(1)
+        load_x(0)
+        load_a(2)
+        load_x(1)
+        load_a(3)
+        load_b(1)
+        load_x(2)
+        load_x(3)
+        load_b(2)
+        load_b(3)
+
+        nc.vector.tensor_copy(out=da_f[:], in_=da_b[:])
+        for t in range(4):
+            nc.vector.tensor_scalar_mul(out=diag[:, t, :], in0=ident_b[:], scalar1=da_f[:, t : t + 1])
+        for c in range(NOC):
+            bank = ps_wk.tile([P, CH], F32, name="bank_db", tag="wk")
+            nc.tensor.matmul(out=bank[:], lhsT=ones[:], rhs=zrow[:, c * CH : (c + 1) * CH], start=True, stop=True)
+            nc.vector.tensor_copy(out=db_bc[:, c * CH : (c + 1) * CH], in_=bank[:])
+
+        sa_c = [keep.tile([P, CH], U32, name="sa_c%d" % g, align_bytes=64) for g in range(NG)]
+        sa_s = [keep.tile([P, CH], U8, name="sa_s%d" % g, align_bytes=64) for g in range(NG)]
+        x_c = [keep.tile([P, TOK], U32, name="x_c%d" % g, align_bytes=64) for g in range(NG)]
+        x_s = [keep.tile([P, TOK], U8, name="x_s%d" % g, align_bytes=64) for g in range(NG)]
+        bt_c = [keep.tile([P, CH], U32, name="bt_c%d" % c, align_bytes=64) for c in range(NOC)]
+        bt_s = [keep.tile([P, CH], U8, name="bt_s%d" % c, align_bytes=64) for c in range(NOC)]
+
+        def copy_out(eng, dst, src):
+            if eng == "v":
+                nc.vector.tensor_copy(out=dst, in_=src)
+            else:
+                nc.scalar.copy(out=dst, in_=src)
+
+        def prep_a(g, engs):
+            ga = grp.tile([P, 4 * CH], BF16, name="ga", tag="grp", align_bytes=64)
+            for cb in range(4):
+                u, e = cb // 2, cb % 2
+                bank = ps_wk.tile([P, 4, P], F32, name="bank_a", tag="wk")
+                for t in range(4):
+                    cols = a_raw[g][:, t, :].rearrange("p (u c e) -> p u e c", u=2, e=2)[:, u, e, :]
+                    nc.tensor.matmul(out=bank[:, t, :], lhsT=diag[:, t, :], rhs=cols, start=True, stop=True)
+                copy_out(
+                    engs[cb],
+                    ga[:, cb * CH : (cb + 1) * CH].rearrange("p (c t) -> p c t", t=4),
+                    bank[:].rearrange("p t c -> p c t"),
+                )
+            nc.vector.quantize_mx(out=sa_c[g][:].bitcast(FP8X4), scales=sa_s[g][:], in_=ga[:])
+
+        def prep_klast(src, codes, scales, engs):
+            gk = grp.tile([P, 4 * CH], BF16, name="gk", tag="grp", align_bytes=64)
+            src32 = src[:].bitcast(F32)
+            gk32 = gk[:].bitcast(F32)
+            for half in range(2):
+                bank = ps_wk.tile([P, 2, 2, P], F32, name="bank_t", tag="wk")
+                for j in range(2):
+                    for u in range(2):
+                        w0 = (2 * half + j) * 256 + u * P
+                        nc.tensor.transpose(bank[:, j, u, :], src32[:, w0 : w0 + P], ident_f[:])
+                copy_out(
+                    engs[half],
+                    gk32[:, half * CH : (half + 1) * CH].rearrange("p (j o u) -> p j o u", j=2, u=2),
+                    bank[:].rearrange("p j u o -> p j o u"),
+                )
+            nc.vector.quantize_mx(out=codes[:].bitcast(FP8X4), scales=scales[:], in_=gk[:])
+
+        def prep_x(g, engs):
+            prep_klast(x_raw[g], x_c[g], x_s[g], engs)
+
+        def prep_b(c, engs):
+            prep_klast(b_raw[c], bt_c[c], bt_s[c], engs)
+
+        state = {}
+
+        def w_bank(unit, ob):
+            oc, g = unit // NG, unit % NG
+            if ob == 0:
+                state["wg%d" % unit] = wgp.tile([P, 4 * CH], BF16, name="wg", tag="wg", align_bytes=64)
+            wg = state["wg%d" % unit]
+            bank = ps_wk.tile([P, 4, P], F32, name="bank_w", tag="wk")
+            for t in range(4):
+                nc.tensor.matmul_mx(
+                    out=bank[:, t, :],
+                    lhsT=sa_c[g][:, t * P : (t + 1) * P].bitcast(FP8X4),
+                    lhsT_scale=sa_s[g][:, t * P : (t + 1) * P],
+                    rhs=bt_c[oc][:, ob * P : (ob + 1) * P].bitcast(FP8X4),
+                    rhs_scale=bt_s[oc][:, ob * P : (ob + 1) * P],
+                    start=True,
+                    stop=True,
+                )
+            o0 = oc * CH + ob * P
+            nc.vector.tensor_tensor(
+                out=wg[:, ob * CH : (ob + 1) * CH].rearrange("p (o t) -> p o t", t=4),
+                in0=bank[:].rearrange("p t o -> p o t"),
+                in1=db_bc[:, o0 : o0 + P].unsqueeze(2).to_broadcast([P, P, 4]),
+                op=MULT,
+            )
+
+        def finish_unit(unit):
+            oc, g = unit // NG, unit % NG
+            wg = state["wg%d" % unit]
+            w_c = wcp.tile([P, CH], U32, name="w_c", tag="w_c", align_bytes=64)
+            w_s = wcp.tile([P, CH], U8, name="w_s", tag="w_s", align_bytes=64)
+            nc.vector.quantize_mx(out=w_c[:].bitcast(FP8X4), scales=w_s[:], in_=wg[:])
+            if g == 0:
+                for tt in range(4):
+                    state["acc%d" % tt] = ps_acc.tile([P, CH], F32, name="acc%d" % tt, tag="acc%d" % tt)
+            for tt in range(4):
+                nc.tensor.matmul_mx(
+                    out=state["acc%d" % tt][:],
+                    lhsT=x_c[g][:, tt * P : (tt + 1) * P].bitcast(FP8X4),
+                    lhsT_scale=x_s[g][:, tt * P : (tt + 1) * P],
+                    rhs=w_c[:].bitcast(FP8X4),
+                    rhs_scale=w_s[:],
+                    start=(g == 0),
+                    stop=(g == NG - 1),
+                )
+            if g == NG - 1:
+                for tt in range(4):
+                    o_sb = outp.tile([P, CH], F32, name="o_sb", tag="o_sb")
+                    if oc == NOC - 1 and tt % 2 == 1:
+                        nc.vector.tensor_scalar_mul(out=o_sb[:], in0=state["acc%d" % tt][:], scalar1=SCALE)
+                    else:
+                        nc.scalar.activation(out=o_sb[:], in_=state["acc%d" % tt][:], func=COPY, scale=SCALE)
+                    nc.sync.dma_start(
+                        out=out_v[tt * P : (tt + 1) * P, oc * CH : (oc + 1) * CH], in_=o_sb[:]
+                    )
+
+        before = {
+            0: [("a", 0, "vsvs"), ("b", 0, "vs")],
+            1: [("a", 1, "ssss"), ("x", 0, "ss")],
+            2: [("a", 2, "ssss"), ("x", 1, "ss")],
+            3: [("a", 3, "ssss"), ("b", 1, "ss"), ("x", 2, "ss")],
+            4: [("x", 3, "ss")],
+            6: [("b", 2, "ss")],
+            10: [("b", 3, "ss")],
+        }
+        n_units = NOC * NG
+        for unit in range(n_units):
+            for kind, idx, engs in before.get(unit, []):
+                if kind == "a":
+                    prep_a(idx, engs)
+                elif kind == "b":
+                    prep_b(idx, engs)
+                else:
+                    prep_x(idx, engs)
+            for ob in range(4):
+                w_bank(unit, ob)
+                if ob == 0 and unit > 0:
+                    finish_unit(unit - 1)
+        finish_unit(n_units - 1)

@@ -16,6 +16,7 @@ TOK, DI, DO, R = 512, 2048, 2048, 512
 CH = 512
 NG = DI // CH
 NOC = DO // CH
+N_UNITS = NOC * NG
 SCALE = 0.125
 FLOPS = 2 * DO * DI * R + 2 * TOK * DI * DO
 
@@ -26,36 +27,23 @@ def tile_veralayer_pa_kernel(tc, x, A, B, d_A, d_B, out):
         const = ctx.enter_context(tc.tile_pool(name="const", bufs=1))
         raw = ctx.enter_context(tc.tile_pool(name="raw", bufs=1))
         keep = ctx.enter_context(tc.tile_pool(name="keep", bufs=1))
-        grp = ctx.enter_context(tc.tile_pool(name="grp", bufs=3))
+        grp = ctx.enter_context(tc.tile_pool(name="grp", bufs=4))
         wgp = ctx.enter_context(tc.tile_pool(name="wgp", bufs=3))
-        wcp = ctx.enter_context(tc.tile_pool(name="wcp", bufs=3))
-        outp = ctx.enter_context(tc.tile_pool(name="outp", bufs=4))
-        ps_wk = ctx.enter_context(tc.psum_pool(name="ps_wk", bufs=4))
-        ps_acc = ctx.enter_context(tc.psum_pool(name="ps_acc", bufs=1))
+        outp = ctx.enter_context(tc.tile_pool(name="outp", bufs=6))
+        ps_w = ctx.enter_context(tc.psum_pool(name="ps_w", bufs=3))
+        ps_o = ctx.enter_context(tc.psum_pool(name="ps_o", bufs=5))
 
         x_v = x.rearrange("b s i -> (b s) i").rearrange("(tt p) i -> p tt i", p=P)
         out_v = out.rearrange("b s o -> (b s) o")
         a_v = A.rearrange("(u p e) i -> u p e i", u=2, e=2)
         b_v = B.rearrange("(ot p) r -> p ot r", p=P)
 
-        zrow = const.tile([P, DO], BF16)
-        ones = const.tile([P, P], BF16)
-        ident_f = const.tile([P, P], F32)
-        ident_b = const.tile([P, P], BF16)
-        da_b = const.tile([P, 4], BF16)
-        da_f = const.tile([P, 4], F32)
-        diag = const.tile([P, 4, P], BF16)
-        db_bc = const.tile([P, DO], BF16)
-
-        nc.scalar.dma_start(
-            out=da_b[:].rearrange("p (u e) -> p u e", u=2),
-            in_=d_A.rearrange("(u p e) -> p u e", u=2, e=2),
-        )
-        nc.vector.memset(zrow[:], 0.0)
-        nc.scalar.dma_start(out=zrow[0:1, :], in_=d_B.rearrange("(a n) -> a n", a=1))
-        nc.vector.memset(ones[:], 1.0)
-        make_identity(nc, ident_b[:])
-        make_identity(nc, ident_f[:])
+        ident_f = const.tile([P, P], F32, name="ident_f")
+        ident_b = const.tile([P, P], BF16, name="ident_b")
+        da_b = const.tile([P, 4], BF16, name="da_b")
+        da_f = const.tile([P, 4], F32, name="da_f")
+        diag = const.tile([P, 4, P], BF16, name="diag")
+        db_bc = const.tile([P, DO], BF16, name="db_bc")
 
         a_raw = [raw.tile([P, 4, CH], BF16, name="a_raw%d" % g) for g in range(NG)]
         x_raw = [raw.tile([P, 4 * CH], BF16, name="x_raw%d" % g) for g in range(NG)]
@@ -63,30 +51,31 @@ def tile_veralayer_pa_kernel(tc, x, A, B, d_A, d_B, out):
 
         def load_a(g):
             for u in range(2):
-                nc.sync.dma_start(
-                    out=a_raw[g][:, 2 * u : 2 * u + 2, :],
-                    in_=a_v[u][:, :, g * CH : (g + 1) * CH],
-                )
+                nc.sync.dma_start(out=a_raw[g][:, 2 * u : 2 * u + 2, :], in_=a_v[u][:, :, g * CH : (g + 1) * CH])
 
         def load_x(g):
             nc.sync.dma_start(
-                out=x_raw[g][:].rearrange("p (tt i) -> p tt i", tt=4),
-                in_=x_v[:, :, g * CH : (g + 1) * CH],
+                out=x_raw[g][:].rearrange("p (tt i) -> p tt i", tt=4), in_=x_v[:, :, g * CH : (g + 1) * CH]
             )
 
         def load_b(c):
             nc.sync.dma_start(
-                out=b_raw[c][:].rearrange("p (ot r) -> p ot r", ot=4),
-                in_=b_v[:, 4 * c : 4 * c + 4, :],
+                out=b_raw[c][:].rearrange("p (ot r) -> p ot r", ot=4), in_=b_v[:, 4 * c : 4 * c + 4, :]
             )
 
+        nc.sync.dma_start(
+            out=da_b[:].rearrange("p (u e) -> p u e", u=2), in_=d_A.rearrange("(u p e) -> p u e", u=2, e=2)
+        )
+        make_identity(nc, ident_b[:])
+        make_identity(nc, ident_f[:])
         load_a(0)
         load_b(0)
+        nc.sync.dma_start(out=db_bc[:], in_=d_B.partition_broadcast(P))
         load_a(1)
-        load_x(0)
         load_a(2)
-        load_x(1)
+        load_x(0)
         load_a(3)
+        load_x(1)
         load_b(1)
         load_x(2)
         load_x(3)
@@ -96,10 +85,6 @@ def tile_veralayer_pa_kernel(tc, x, A, B, d_A, d_B, out):
         nc.vector.tensor_copy(out=da_f[:], in_=da_b[:])
         for t in range(4):
             nc.vector.tensor_scalar_mul(out=diag[:, t, :], in0=ident_b[:], scalar1=da_f[:, t : t + 1])
-        for c in range(NOC):
-            bank = ps_wk.tile([P, CH], F32, name="bank_db", tag="wk")
-            nc.tensor.matmul(out=bank[:], lhsT=ones[:], rhs=zrow[:, c * CH : (c + 1) * CH], start=True, stop=True)
-            nc.vector.tensor_copy(out=db_bc[:, c * CH : (c + 1) * CH], in_=bank[:])
 
         sa_c = [keep.tile([P, CH], U32, name="sa_c%d" % g, align_bytes=64) for g in range(NG)]
         sa_s = [keep.tile([P, CH], U8, name="sa_s%d" % g, align_bytes=64) for g in range(NG)]
@@ -107,6 +92,10 @@ def tile_veralayer_pa_kernel(tc, x, A, B, d_A, d_B, out):
         x_s = [keep.tile([P, TOK], U8, name="x_s%d" % g, align_bytes=64) for g in range(NG)]
         bt_c = [keep.tile([P, CH], U32, name="bt_c%d" % c, align_bytes=64) for c in range(NOC)]
         bt_s = [keep.tile([P, CH], U8, name="bt_s%d" % c, align_bytes=64) for c in range(NOC)]
+        w_c = [keep.tile([P, CH], U32, name="w_c%d" % n, align_bytes=64) for n in range(N_UNITS)]
+        w_s = [keep.tile([P, CH], U8, name="w_s%d" % n, align_bytes=64) for n in range(N_UNITS)]
+
+        acc = {}
 
         def copy_out(eng, dst, src):
             if eng == "v":
@@ -118,7 +107,7 @@ def tile_veralayer_pa_kernel(tc, x, A, B, d_A, d_B, out):
             ga = grp.tile([P, 4 * CH], BF16, name="ga", tag="grp", align_bytes=64)
             for cb in range(4):
                 u, e = cb // 2, cb % 2
-                bank = ps_wk.tile([P, 4, P], F32, name="bank_a", tag="wk")
+                bank = ps_o.tile([P, 4, P], F32, name="bank_a", tag="o")
                 for t in range(4):
                     cols = a_raw[g][:, t, :].rearrange("p (u c e) -> p u e c", u=2, e=2)[:, u, e, :]
                     nc.tensor.matmul(out=bank[:, t, :], lhsT=diag[:, t, :], rhs=cols, start=True, stop=True)
@@ -129,12 +118,12 @@ def tile_veralayer_pa_kernel(tc, x, A, B, d_A, d_B, out):
                 )
             nc.vector.quantize_mx(out=sa_c[g][:].bitcast(FP8X4), scales=sa_s[g][:], in_=ga[:])
 
-        def prep_klast(src, codes, scales, engs):
+        def prep_t(src, codes, scales, engs):
             gk = grp.tile([P, 4 * CH], BF16, name="gk", tag="grp", align_bytes=64)
             src32 = src[:].bitcast(F32)
             gk32 = gk[:].bitcast(F32)
             for half in range(2):
-                bank = ps_wk.tile([P, 2, 2, P], F32, name="bank_t", tag="wk")
+                bank = ps_o.tile([P, 2, 2, P], F32, name="bank_t", tag="o")
                 for j in range(2):
                     for u in range(2):
                         w0 = (2 * half + j) * 256 + u * P
@@ -146,88 +135,90 @@ def tile_veralayer_pa_kernel(tc, x, A, B, d_A, d_B, out):
                 )
             nc.vector.quantize_mx(out=codes[:].bitcast(FP8X4), scales=scales[:], in_=gk[:])
 
-        def prep_x(g, engs):
-            prep_klast(x_raw[g], x_c[g], x_s[g], engs)
+        def prep_x(g):
+            prep_t(x_raw[g], x_c[g], x_s[g], "ss")
 
         def prep_b(c, engs):
-            prep_klast(b_raw[c], bt_c[c], bt_s[c], engs)
+            prep_t(b_raw[c], bt_c[c], bt_s[c], engs)
 
-        state = {}
+        def db_view(o0):
+            return db_bc[:, o0 : o0 + P].unsqueeze(2).to_broadcast([P, P, 4])
 
-        def w_bank(unit, ob):
-            oc, g = unit // NG, unit % NG
-            if ob == 0:
-                state["wg%d" % unit] = wgp.tile([P, 4 * CH], BF16, name="wg", tag="wg", align_bytes=64)
-            wg = state["wg%d" % unit]
-            bank = ps_wk.tile([P, 4, P], F32, name="bank_w", tag="wk")
-            for t in range(4):
-                nc.tensor.matmul_mx(
-                    out=bank[:, t, :],
-                    lhsT=sa_c[g][:, t * P : (t + 1) * P].bitcast(FP8X4),
-                    lhsT_scale=sa_s[g][:, t * P : (t + 1) * P],
-                    rhs=bt_c[oc][:, ob * P : (ob + 1) * P].bitcast(FP8X4),
-                    rhs_scale=bt_s[oc][:, ob * P : (ob + 1) * P],
-                    start=True,
-                    stop=True,
-                )
-            o0 = oc * CH + ob * P
-            nc.vector.tensor_tensor(
-                out=wg[:, ob * CH : (ob + 1) * CH].rearrange("p (o t) -> p o t", t=4),
-                in0=bank[:].rearrange("p t o -> p o t"),
-                in1=db_bc[:, o0 : o0 + P].unsqueeze(2).to_broadcast([P, P, 4]),
-                op=MULT,
-            )
+        def w_unit(n):
+            oc, g = n // NG, n % NG
+            wgv = wgp.tile([P, 3 * CH], BF16, name="wgv", tag="wgv", align_bytes=64)
+            wgg = wgp.tile([P, CH], BF16, name="wgg", tag="wgg", align_bytes=64)
+            for ob in range(4):
+                bank = ps_w.tile([P, 4, P], F32, name="bank_w", tag="w")
+                for t in range(4):
+                    nc.tensor.matmul_mx(
+                        out=bank[:, t, :],
+                        lhsT=sa_c[g][:, t * P : (t + 1) * P].bitcast(FP8X4),
+                        lhsT_scale=sa_s[g][:, t * P : (t + 1) * P],
+                        rhs=bt_c[oc][:, ob * P : (ob + 1) * P].bitcast(FP8X4),
+                        rhs_scale=bt_s[oc][:, ob * P : (ob + 1) * P],
+                        start=True,
+                        stop=True,
+                    )
+                o0 = oc * CH + ob * P
+                if ob == 0:
+                    wf = wgp.tile([P, CH], F32, name="wf", tag="wf")
+                    nc.scalar.copy(out=wf[:].rearrange("p (o t) -> p o t", t=4), in_=bank[:].rearrange("p t o -> p o t"))
+                    nc.gpsimd.tensor_tensor(
+                        out=wgg[:].rearrange("p (o t) -> p o t", t=4),
+                        in0=wf[:].rearrange("p (o t) -> p o t", t=4),
+                        in1=db_view(o0),
+                        op=MULT,
+                    )
+                else:
+                    nc.vector.tensor_tensor(
+                        out=wgv[:, (ob - 1) * CH : ob * CH].rearrange("p (o t) -> p o t", t=4),
+                        in0=bank[:].rearrange("p t o -> p o t"),
+                        in1=db_view(o0),
+                        op=MULT,
+                    )
+            for lo, hi, src in ((P, 3 * P, wgv[:, 0 : 2 * CH]), (3 * P, 4 * P, wgv[:, 2 * CH : 3 * CH]), (0, P, wgg[:])):
+                nc.vector.quantize_mx(out=w_c[n][:, lo:hi].bitcast(FP8X4), scales=w_s[n][:, lo:hi], in_=src)
 
-        def finish_unit(unit):
-            oc, g = unit // NG, unit % NG
-            wg = state["wg%d" % unit]
-            w_c = wcp.tile([P, CH], U32, name="w_c", tag="w_c", align_bytes=64)
-            w_s = wcp.tile([P, CH], U8, name="w_s", tag="w_s", align_bytes=64)
-            nc.vector.quantize_mx(out=w_c[:].bitcast(FP8X4), scales=w_s[:], in_=wg[:])
+        def second(n):
+            oc, g = n // NG, n % NG
             if g == 0:
                 for tt in range(4):
-                    state["acc%d" % tt] = ps_acc.tile([P, CH], F32, name="acc%d" % tt, tag="acc%d" % tt)
+                    acc[(oc, tt)] = ps_o.tile([P, CH], F32, name="acc", tag="o")
             for tt in range(4):
                 nc.tensor.matmul_mx(
-                    out=state["acc%d" % tt][:],
+                    out=acc[(oc, tt)][:],
                     lhsT=x_c[g][:, tt * P : (tt + 1) * P].bitcast(FP8X4),
                     lhsT_scale=x_s[g][:, tt * P : (tt + 1) * P],
-                    rhs=w_c[:].bitcast(FP8X4),
-                    rhs_scale=w_s[:],
+                    rhs=w_c[n][:].bitcast(FP8X4),
+                    rhs_scale=w_s[n][:],
                     start=(g == 0),
                     stop=(g == NG - 1),
                 )
-            if g == NG - 1:
-                for tt in range(4):
-                    o_sb = outp.tile([P, CH], F32, name="o_sb", tag="o_sb")
-                    if oc == NOC - 1 and tt % 2 == 1:
-                        nc.vector.tensor_scalar_mul(out=o_sb[:], in0=state["acc%d" % tt][:], scalar1=SCALE)
-                    else:
-                        nc.scalar.activation(out=o_sb[:], in_=state["acc%d" % tt][:], func=COPY, scale=SCALE)
-                    nc.sync.dma_start(
-                        out=out_v[tt * P : (tt + 1) * P, oc * CH : (oc + 1) * CH], in_=o_sb[:]
-                    )
 
-        before = {
-            0: [("a", 0, "vsvs"), ("b", 0, "vs")],
-            1: [("a", 1, "ssss"), ("x", 0, "ss")],
-            2: [("a", 2, "ssss"), ("x", 1, "ss")],
-            3: [("a", 3, "ssss"), ("b", 1, "ss"), ("x", 2, "ss")],
-            4: [("x", 3, "ss")],
-            6: [("b", 2, "ss")],
-            10: [("b", 3, "ss")],
-        }
-        n_units = NOC * NG
-        for unit in range(n_units):
-            for kind, idx, engs in before.get(unit, []):
-                if kind == "a":
-                    prep_a(idx, engs)
-                elif kind == "b":
-                    prep_b(idx, engs)
+        def store_out(oc, engs):
+            for tt in range(4):
+                o_sb = outp.tile([P, CH], F32, name="o_sb", tag="o_sb")
+                if engs[tt] == "v":
+                    nc.vector.tensor_scalar_mul(out=o_sb[:], in0=acc[(oc, tt)][:], scalar1=SCALE)
                 else:
-                    prep_x(idx, engs)
-            for ob in range(4):
-                w_bank(unit, ob)
-                if ob == 0 and unit > 0:
-                    finish_unit(unit - 1)
-        finish_unit(n_units - 1)
+                    nc.scalar.activation(out=o_sb[:], in_=acc[(oc, tt)][:], func=COPY, scale=SCALE)
+                nc.sync.dma_start(out=out_v[tt * P : (tt + 1) * P, oc * CH : (oc + 1) * CH], in_=o_sb[:])
+
+        prep_a(0, "vsvs")
+        prep_b(0, "vs")
+        prep_a(1, "ssss")
+        prep_a(2, "ssss")
+        prep_a(3, "ssss")
+        for n in range(N_UNITS):
+            w_unit(n)
+            if n < NG:
+                prep_x(n)
+            if n % NG == 1 and n // NG + 1 < NOC:
+                prep_b(n // NG + 1, "ss")
+            if n >= 2 and (n - 2) % NG == NG - 1:
+                store_out((n - 2) // NG, "ssss")
+            if n >= 1:
+                second(n - 1)
+        second(N_UNITS - 1)
+        store_out(NOC - 1, "svsv")

@@ -9,6 +9,7 @@ U32 = mybir.dt.uint32
 U8 = mybir.dt.uint8
 FP8X4 = mybir.dt.float8_e4m3fn_x4
 MULT = mybir.AluOpType.mult
+ADD = mybir.AluOpType.add
 COPY = mybir.ActivationFunctionType.Copy
 
 P = 128
@@ -39,11 +40,9 @@ def tile_veralayer_pa_kernel(tc, x, A, B, d_A, d_B, out):
         b_v = B.rearrange("(ot p) r -> p ot r", p=P)
 
         ident_f = const.tile([P, P], F32, name="ident_f")
-        ident_b = const.tile([P, P], BF16, name="ident_b")
         da_b = const.tile([P, 4], BF16, name="da_b")
         da_f = const.tile([P, 4], F32, name="da_f")
-        diag = const.tile([P, 4, P], BF16, name="diag")
-        db_bc = const.tile([P, DO], BF16, name="db_bc")
+        db_bc = [const.tile([P, CH], BF16, name="db_bc%d" % c) for c in range(NOC)]
 
         a_raw = [raw.tile([P, 4, CH], BF16, name="a_raw%d" % g) for g in range(NG)]
         x_raw = [raw.tile([P, 4 * CH], BF16, name="x_raw%d" % g) for g in range(NG)]
@@ -66,25 +65,25 @@ def tile_veralayer_pa_kernel(tc, x, A, B, d_A, d_B, out):
         nc.sync.dma_start(
             out=da_b[:].rearrange("p (u e) -> p u e", u=2), in_=d_A.rearrange("(u p e) -> p u e", u=2, e=2)
         )
-        make_identity(nc, ident_b[:])
         make_identity(nc, ident_f[:])
         load_a(0)
         load_b(0)
-        nc.sync.dma_start(out=db_bc[:], in_=d_B.partition_broadcast(P))
         load_a(1)
+        nc.sync.dma_start(out=db_bc[0][:], in_=d_B[0 * CH : 1 * CH].partition_broadcast(P))
         load_a(2)
-        load_x(0)
         load_a(3)
+        load_x(0)
+        nc.sync.dma_start(out=db_bc[1][:], in_=d_B[1 * CH : 2 * CH].partition_broadcast(P))
         load_x(1)
         load_b(1)
         load_x(2)
         load_x(3)
+        nc.sync.dma_start(out=db_bc[2][:], in_=d_B[2 * CH : 3 * CH].partition_broadcast(P))
         load_b(2)
+        nc.sync.dma_start(out=db_bc[3][:], in_=d_B[3 * CH : 4 * CH].partition_broadcast(P))
         load_b(3)
 
         nc.vector.tensor_copy(out=da_f[:], in_=da_b[:])
-        for t in range(4):
-            nc.vector.tensor_scalar_mul(out=diag[:, t, :], in0=ident_b[:], scalar1=da_f[:, t : t + 1])
 
         sa_c = [keep.tile([P, CH], U32, name="sa_c%d" % g, align_bytes=64) for g in range(NG)]
         sa_s = [keep.tile([P, CH], U8, name="sa_s%d" % g, align_bytes=64) for g in range(NG)]
@@ -104,17 +103,17 @@ def tile_veralayer_pa_kernel(tc, x, A, B, d_A, d_B, out):
                 nc.scalar.copy(out=dst, in_=src)
 
         def prep_a(g, engs):
+            a_sc = grp.tile([P, 4, CH], BF16, name="a_sc", tag="a_sc")
+            for t in range(4):
+                nc.vector.tensor_scalar(
+                    out=a_sc[:, t, :], in0=a_raw[g][:, t, :], scalar1=da_f[:, t : t + 1], scalar2=0.0, op0=MULT, op1=ADD
+                )
             ga = grp.tile([P, 4 * CH], BF16, name="ga", tag="grp", align_bytes=64)
-            for cb in range(4):
-                u, e = cb // 2, cb % 2
-                bank = ps_o.tile([P, 4, P], F32, name="bank_a", tag="o")
-                for t in range(4):
-                    cols = a_raw[g][:, t, :].rearrange("p (u c e) -> p u e c", u=2, e=2)[:, u, e, :]
-                    nc.tensor.matmul(out=bank[:, t, :], lhsT=diag[:, t, :], rhs=cols, start=True, stop=True)
+            for u in range(2):
                 copy_out(
-                    engs[cb],
-                    ga[:, cb * CH : (cb + 1) * CH].rearrange("p (c t) -> p c t", t=4),
-                    bank[:].rearrange("p t c -> p c t"),
+                    engs[u],
+                    ga[:, 2 * u * CH : 2 * (u + 1) * CH].rearrange("p (e c t) -> p e c t", e=2, t=4),
+                    a_sc[:].rearrange("p t (u c e) -> p u e c t", u=2, e=2)[:, u],
                 )
             nc.vector.quantize_mx(out=sa_c[g][:].bitcast(FP8X4), scales=sa_s[g][:], in_=ga[:])
 
@@ -142,7 +141,7 @@ def tile_veralayer_pa_kernel(tc, x, A, B, d_A, d_B, out):
             prep_t(b_raw[c], bt_c[c], bt_s[c], engs)
 
         def db_view(o0):
-            return db_bc[:, o0 : o0 + P].unsqueeze(2).to_broadcast([P, P, 4])
+            return db_bc[o0 // CH][:, o0 % CH : o0 % CH + P].unsqueeze(2).to_broadcast([P, P, 4])
 
         def w_unit(n):
             oc, g = n // NG, n % NG
@@ -205,13 +204,13 @@ def tile_veralayer_pa_kernel(tc, x, A, B, d_A, d_B, out):
                     nc.scalar.activation(out=o_sb[:], in_=acc[(oc, tt)][:], func=COPY, scale=SCALE)
                 nc.sync.dma_start(out=out_v[tt * P : (tt + 1) * P, oc * CH : (oc + 1) * CH], in_=o_sb[:])
 
-        prep_a(0, "vsvs")
+        prep_a(0, "vs")
         prep_b(0, "vs")
-        prep_a(1, "ssss")
-        prep_a(2, "ssss")
-        prep_a(3, "ssss")
+        prep_a(1, "ss")
         for n in range(N_UNITS):
             w_unit(n)
+            if n + 2 < NG:
+                prep_a(n + 2, "ss")
             if n < NG:
                 prep_x(n)
             if n % NG == 1 and n // NG + 1 < NOC:

@@ -31,8 +31,8 @@ def tile_veralayer_pa_kernel(tc, x, A, B, d_A, d_B, out):
         grp = ctx.enter_context(tc.tile_pool(name="grp", bufs=4))
         wgp = ctx.enter_context(tc.tile_pool(name="wgp", bufs=3))
         outp = ctx.enter_context(tc.tile_pool(name="outp", bufs=6))
-        ps_w = ctx.enter_context(tc.psum_pool(name="ps_w", bufs=3))
-        ps_o = ctx.enter_context(tc.psum_pool(name="ps_o", bufs=5))
+        ps_w = ctx.enter_context(tc.psum_pool(name="ps_w", bufs=4))
+        ps_o = ctx.enter_context(tc.psum_pool(name="ps_o", bufs=4))
 
         x_v = x.rearrange("b s i -> (b s) i").rearrange("(tt p) i -> p tt i", p=P)
         out_v = out.rearrange("b s o -> (b s) o")
@@ -122,7 +122,7 @@ def tile_veralayer_pa_kernel(tc, x, A, B, d_A, d_B, out):
             src32 = src[:].bitcast(F32)
             gk32 = gk[:].bitcast(F32)
             for half in range(2):
-                bank = ps_o.tile([P, 2, 2, P], F32, name="bank_t", tag="o")
+                bank = ps_w.tile([P, 2, 2, P], F32, name="bank_t", tag="w")
                 for j in range(2):
                     for u in range(2):
                         w0 = (2 * half + j) * 256 + u * P
@@ -146,7 +146,7 @@ def tile_veralayer_pa_kernel(tc, x, A, B, d_A, d_B, out):
         def w_unit(n):
             oc, g = n // NG, n % NG
             wgv = wgp.tile([P, 3 * CH], BF16, name="wgv", tag="wgv", align_bytes=64)
-            wgg = wgp.tile([P, CH], BF16, name="wgg", tag="wgg", align_bytes=64)
+            wgg = wgp.tile([P, CH], BF16, name="wgg", tag="wgg", bufs=1, align_bytes=64)
             for ob in range(4):
                 bank = ps_w.tile([P, 4, P], F32, name="bank_w", tag="w")
                 for t in range(4):

@@ -19,20 +19,23 @@ NG = DI // CH
 NOC = DO // CH
 N_UNITS = NOC * NG
 SCALE = 0.125
+LAG = 3
+G0 = 0
 FLOPS = 2 * DO * DI * R + 2 * TOK * DI * DO
 
 
 def tile_veralayer_pa_kernel(tc, x, A, B, d_A, d_B, out):
     nc = tc.nc
     with ExitStack() as ctx:
+        ctx.enter_context(tc.manual_schedule())
         const = ctx.enter_context(tc.tile_pool(name="const", bufs=1))
         raw = ctx.enter_context(tc.tile_pool(name="raw", bufs=1))
         keep = ctx.enter_context(tc.tile_pool(name="keep", bufs=1))
         grp = ctx.enter_context(tc.tile_pool(name="grp", bufs=4))
-        wgp = ctx.enter_context(tc.tile_pool(name="wgp", bufs=3))
+        wgp = ctx.enter_context(tc.tile_pool(name="wgp", bufs=2))
         outp = ctx.enter_context(tc.tile_pool(name="outp", bufs=6))
         ps_w = ctx.enter_context(tc.psum_pool(name="ps_w", bufs=4))
-        ps_o = ctx.enter_context(tc.psum_pool(name="ps_o", bufs=4))
+        ps_o = ctx.enter_context(tc.psum_pool(name="ps_o", bufs=1))
 
         x_v = x.rearrange("b s i -> (b s) i").rearrange("(tt p) i -> p tt i", p=P)
         out_v = out.rearrange("b s o -> (b s) o")
@@ -43,58 +46,48 @@ def tile_veralayer_pa_kernel(tc, x, A, B, d_A, d_B, out):
         da_b = const.tile([P, 4], BF16, name="da_b")
         da_f = const.tile([P, 4], F32, name="da_f")
         db_bc = [const.tile([P, CH], BF16, name="db_bc%d" % c) for c in range(NOC)]
-
         a_raw = [raw.tile([P, 4, CH], BF16, name="a_raw%d" % g) for g in range(NG)]
         x_raw = [raw.tile([P, 4 * CH], BF16, name="x_raw%d" % g) for g in range(NG)]
         b_raw = [raw.tile([P, 4 * R], BF16, name="b_raw%d" % c) for c in range(NOC)]
 
-        def load_a(g):
-            for u in range(2):
-                nc.sync.dma_start(out=a_raw[g][:, 2 * u : 2 * u + 2, :], in_=a_v[u][:, :, g * CH : (g + 1) * CH])
-
-        def load_x(g):
-            nc.sync.dma_start(
-                out=x_raw[g][:].rearrange("p (tt i) -> p tt i", tt=4), in_=x_v[:, :, g * CH : (g + 1) * CH]
-            )
-
-        def load_b(c):
-            nc.sync.dma_start(
-                out=b_raw[c][:].rearrange("p (ot r) -> p ot r", ot=4), in_=b_v[:, 4 * c : 4 * c + 4, :]
-            )
+        def load(kind, k):
+            if kind == "a":
+                for u in range(2):
+                    nc.sync.dma_start(out=a_raw[k][:, 2 * u : 2 * u + 2, :], in_=a_v[u][:, :, k * CH : (k + 1) * CH])
+            elif kind == "x":
+                nc.sync.dma_start(
+                    out=x_raw[k][:].rearrange("p (tt i) -> p tt i", tt=4), in_=x_v[:, :, k * CH : (k + 1) * CH]
+                )
+            elif kind == "b":
+                nc.sync.dma_start(
+                    out=b_raw[k][:].rearrange("p (ot r) -> p ot r", ot=4), in_=b_v[:, 4 * k : 4 * k + 4, :]
+                )
+            else:
+                nc.sync.dma_start(out=db_bc[k][:], in_=d_B[k * CH : (k + 1) * CH].partition_broadcast(P))
 
         nc.sync.dma_start(
             out=da_b[:].rearrange("p (u e) -> p u e", u=2), in_=d_A.rearrange("(u p e) -> p u e", u=2, e=2)
         )
         make_identity(nc, ident_f[:])
-        load_a(0)
-        load_b(0)
-        load_a(1)
-        nc.sync.dma_start(out=db_bc[0][:], in_=d_B[0 * CH : 1 * CH].partition_broadcast(P))
-        load_a(2)
-        load_a(3)
-        load_x(0)
-        nc.sync.dma_start(out=db_bc[1][:], in_=d_B[1 * CH : 2 * CH].partition_broadcast(P))
-        load_x(1)
-        load_b(1)
-        load_x(2)
-        load_x(3)
-        nc.sync.dma_start(out=db_bc[2][:], in_=d_B[2 * CH : 3 * CH].partition_broadcast(P))
-        load_b(2)
-        nc.sync.dma_start(out=db_bc[3][:], in_=d_B[3 * CH : 4 * CH].partition_broadcast(P))
-        load_b(3)
-
+        for kind, k in (("a", 0), ("b", 0), ("a", 1), ("d", 0), ("a", 2), ("x", 0), ("a", 3), ("x", 1), ("d", 1), ("b", 1), ("x", 2), ("x", 3), ("d", 2), ("b", 2), ("d", 3), ("b", 3)):
+            load(kind, k)
         nc.vector.tensor_copy(out=da_f[:], in_=da_b[:])
 
-        sa_c = [keep.tile([P, CH], U32, name="sa_c%d" % g, align_bytes=64) for g in range(NG)]
-        sa_s = [keep.tile([P, CH], U8, name="sa_s%d" % g, align_bytes=64) for g in range(NG)]
-        x_c = [keep.tile([P, TOK], U32, name="x_c%d" % g, align_bytes=64) for g in range(NG)]
-        x_s = [keep.tile([P, TOK], U8, name="x_s%d" % g, align_bytes=64) for g in range(NG)]
-        bt_c = [keep.tile([P, CH], U32, name="bt_c%d" % c, align_bytes=64) for c in range(NOC)]
-        bt_s = [keep.tile([P, CH], U8, name="bt_s%d" % c, align_bytes=64) for c in range(NOC)]
-        w_c = [keep.tile([P, CH], U32, name="w_c%d" % n, align_bytes=64) for n in range(N_UNITS)]
-        w_s = [keep.tile([P, CH], U8, name="w_s%d" % n, align_bytes=64) for n in range(N_UNITS)]
-
+        codes = {}
+        for kind, count in (("a", NG), ("x", NG), ("b", NOC), ("w", N_UNITS)):
+            for k in range(count):
+                codes[(kind, k)] = (
+                    keep.tile([P, CH], U32, name="%s_c%d" % (kind, k), align_bytes=64),
+                    keep.tile([P, CH], U8, name="%s_s%d" % (kind, k), align_bytes=64),
+                )
+        grouped = {}
         acc = {}
+
+        def words(kind, k, lo, hi):
+            return codes[(kind, k)][0][:, lo:hi].bitcast(FP8X4)
+
+        def scales(kind, k, lo, hi):
+            return codes[(kind, k)][1][:, lo:hi]
 
         def copy_out(eng, dst, src):
             if eng == "v":
@@ -102,122 +95,136 @@ def tile_veralayer_pa_kernel(tc, x, A, B, d_A, d_B, out):
             else:
                 nc.scalar.copy(out=dst, in_=src)
 
-        def prep_a(g, engs):
+        def group_a(g, engs):
             a_sc = grp.tile([P, 4, CH], BF16, name="a_sc", tag="a_sc")
             for t in range(4):
                 nc.vector.tensor_scalar(
                     out=a_sc[:, t, :], in0=a_raw[g][:, t, :], scalar1=da_f[:, t : t + 1], scalar2=0.0, op0=MULT, op1=ADD
                 )
             ga = grp.tile([P, 4 * CH], BF16, name="ga", tag="grp", align_bytes=64)
+            grouped[("a", g)] = ga
             for u in range(2):
                 copy_out(
                     engs[u],
                     ga[:, 2 * u * CH : 2 * (u + 1) * CH].rearrange("p (e c t) -> p e c t", e=2, t=4),
                     a_sc[:].rearrange("p t (u c e) -> p u e c t", u=2, e=2)[:, u],
                 )
-            nc.vector.quantize_mx(out=sa_c[g][:].bitcast(FP8X4), scales=sa_s[g][:], in_=ga[:])
 
-        def prep_t(src, codes, scales, engs):
+        def group_t(kind, k, engs):
+            src32 = (x_raw[k] if kind == "x" else b_raw[k])[:].bitcast(F32)
             gk = grp.tile([P, 4 * CH], BF16, name="gk", tag="grp", align_bytes=64)
-            src32 = src[:].bitcast(F32)
+            grouped[(kind, k)] = gk
             gk32 = gk[:].bitcast(F32)
+            banks = [ps_w.tile([P, 2, 2, P], F32, name="bank_t", tag="w") for half in range(2)]
             for half in range(2):
-                bank = ps_w.tile([P, 2, 2, P], F32, name="bank_t", tag="w")
                 for j in range(2):
                     for u in range(2):
                         w0 = (2 * half + j) * 256 + u * P
-                        nc.tensor.transpose(bank[:, j, u, :], src32[:, w0 : w0 + P], ident_f[:])
+                        nc.tensor.transpose(banks[half][:, j, u, :], src32[:, w0 : w0 + P], ident_f[:])
+            for half in range(2):
                 copy_out(
                     engs[half],
                     gk32[:, half * CH : (half + 1) * CH].rearrange("p (j o u) -> p j o u", j=2, u=2),
-                    bank[:].rearrange("p j u o -> p j o u"),
+                    banks[half][:].rearrange("p j u o -> p j o u"),
                 )
-            nc.vector.quantize_mx(out=codes[:].bitcast(FP8X4), scales=scales[:], in_=gk[:])
 
-        def prep_x(g):
-            prep_t(x_raw[g], x_c[g], x_s[g], "ss")
+        def group(kind, k, engs):
+            if kind == "a":
+                group_a(k, engs)
+            else:
+                group_t(kind, k, engs)
 
-        def prep_b(c, engs):
-            prep_t(b_raw[c], bt_c[c], bt_s[c], engs)
+        def quantise(kind, k):
+            nc.vector.quantize_mx(out=words(kind, k, 0, CH), scales=scales(kind, k, 0, CH), in_=grouped[(kind, k)][:])
 
-        def db_view(o0):
-            return db_bc[o0 // CH][:, o0 % CH : o0 % CH + P].unsqueeze(2).to_broadcast([P, P, 4])
-
-        def w_unit(n):
+        def w_banks(n, m):
             oc, g = n // NG, n % NG
-            wgv = wgp.tile([P, 3 * CH], BF16, name="wgv", tag="wgv", align_bytes=64)
-            wgg = wgp.tile([P, CH], BF16, name="wgg", tag="wgg", bufs=1, align_bytes=64)
+            wgv = wgp.tile([P, 4 * CH], BF16, name="wgv", tag="wgv", align_bytes=64)
+            wgg = wgp.tile([P, CH], BF16, name="wgg", tag="wgg", bufs=1, align_bytes=64) if n >= G0 else None
+            grouped[("w", n)] = (wgv, wgg)
             for ob in range(4):
                 bank = ps_w.tile([P, 4, P], F32, name="bank_w", tag="w")
                 for t in range(4):
                     nc.tensor.matmul_mx(
                         out=bank[:, t, :],
-                        lhsT=sa_c[g][:, t * P : (t + 1) * P].bitcast(FP8X4),
-                        lhsT_scale=sa_s[g][:, t * P : (t + 1) * P],
-                        rhs=bt_c[oc][:, ob * P : (ob + 1) * P].bitcast(FP8X4),
-                        rhs_scale=bt_s[oc][:, ob * P : (ob + 1) * P],
+                        lhsT=words("a", g, t * P, (t + 1) * P),
+                        lhsT_scale=scales("a", g, t * P, (t + 1) * P),
+                        rhs=words("b", oc, ob * P, (ob + 1) * P),
+                        rhs_scale=scales("b", oc, ob * P, (ob + 1) * P),
                         start=True,
                         stop=True,
                     )
-                o0 = oc * CH + ob * P
-                if ob == 0:
+                if m is not None:
+                    second_pass(m, ob)
+                db = db_bc[oc][:, ob * P : (ob + 1) * P].unsqueeze(2).to_broadcast([P, P, 4])
+                if ob == 0 and n >= G0:
                     wf = wgp.tile([P, CH], F32, name="wf", tag="wf")
                     nc.scalar.copy(out=wf[:].rearrange("p (o t) -> p o t", t=4), in_=bank[:].rearrange("p t o -> p o t"))
                     nc.gpsimd.tensor_tensor(
                         out=wgg[:].rearrange("p (o t) -> p o t", t=4),
                         in0=wf[:].rearrange("p (o t) -> p o t", t=4),
-                        in1=db_view(o0),
+                        in1=db,
                         op=MULT,
                     )
                 else:
                     nc.vector.tensor_tensor(
-                        out=wgv[:, (ob - 1) * CH : ob * CH].rearrange("p (o t) -> p o t", t=4),
+                        out=wgv[:, ob * CH : (ob + 1) * CH].rearrange("p (o t) -> p o t", t=4),
                         in0=bank[:].rearrange("p t o -> p o t"),
-                        in1=db_view(o0),
+                        in1=db,
                         op=MULT,
                     )
-            for lo, hi, src in ((P, 3 * P, wgv[:, 0 : 2 * CH]), (3 * P, 4 * P, wgv[:, 2 * CH : 3 * CH]), (0, P, wgg[:])):
-                nc.vector.quantize_mx(out=w_c[n][:, lo:hi].bitcast(FP8X4), scales=w_s[n][:, lo:hi], in_=src)
 
-        def second(n):
+        def w_quantise(n):
+            wgv, wgg = grouped[("w", n)]
+            if n < G0:
+                nc.vector.quantize_mx(out=words("w", n, 0, CH), scales=scales("w", n, 0, CH), in_=wgv[:])
+                return
+            for lo, hi, src in ((P, 3 * P, wgv[:, CH : 3 * CH]), (3 * P, 4 * P, wgv[:, 3 * CH : 4 * CH]), (0, P, wgg[:])):
+                nc.vector.quantize_mx(out=words("w", n, lo, hi), scales=scales("w", n, lo, hi), in_=src)
+
+        def second_pass(n, tt):
             oc, g = n // NG, n % NG
             if g == 0:
-                for tt in range(4):
-                    acc[(oc, tt)] = ps_o.tile([P, CH], F32, name="acc", tag="o")
-            for tt in range(4):
-                nc.tensor.matmul_mx(
-                    out=acc[(oc, tt)][:],
-                    lhsT=x_c[g][:, tt * P : (tt + 1) * P].bitcast(FP8X4),
-                    lhsT_scale=x_s[g][:, tt * P : (tt + 1) * P],
-                    rhs=w_c[n][:].bitcast(FP8X4),
-                    rhs_scale=w_s[n][:],
-                    start=(g == 0),
-                    stop=(g == NG - 1),
-                )
+                acc[tt] = ps_o.tile([P, CH], F32, name="acc%d" % tt, tag="acc%d" % tt)
+            nc.tensor.matmul_mx(
+                out=acc[tt][:],
+                lhsT=words("x", g, tt * P, (tt + 1) * P),
+                lhsT_scale=scales("x", g, tt * P, (tt + 1) * P),
+                rhs=words("w", n, 0, CH),
+                rhs_scale=scales("w", n, 0, CH),
+                start=(g == 0),
+                stop=(g == NG - 1),
+            )
 
         def store_out(oc, engs):
             for tt in range(4):
                 o_sb = outp.tile([P, CH], F32, name="o_sb", tag="o_sb")
                 if engs[tt] == "v":
-                    nc.vector.tensor_scalar_mul(out=o_sb[:], in0=acc[(oc, tt)][:], scalar1=SCALE)
+                    nc.vector.tensor_scalar_mul(out=o_sb[:], in0=acc[tt][:], scalar1=SCALE)
                 else:
-                    nc.scalar.activation(out=o_sb[:], in_=acc[(oc, tt)][:], func=COPY, scale=SCALE)
+                    nc.scalar.activation(out=o_sb[:], in_=acc[tt][:], func=COPY, scale=SCALE)
                 nc.sync.dma_start(out=out_v[tt * P : (tt + 1) * P, oc * CH : (oc + 1) * CH], in_=o_sb[:])
 
-        prep_a(0, "vs")
-        prep_b(0, "vs")
-        prep_a(1, "ss")
+        group("a", 0, "vs")
+        group("b", 0, "vs")
+        quantise("a", 0)
+        quantise("b", 0)
+        pending = [("a", 1), ("a", 2)]
+        for kind, k in pending:
+            group(kind, k, "vs" if kind == "a" else "ss")
+        later = {0: [("x", 0), ("a", 3)], 1: [("x", 1), ("b", 1)], 2: [("x", 2)], 3: [("x", 3)], 5: [("b", 2)], 9: [("b", 3)]}
         for n in range(N_UNITS):
-            w_unit(n)
-            if n + 2 < NG:
-                prep_a(n + 2, "ss")
-            if n < NG:
-                prep_x(n)
-            if n % NG == 1 and n // NG + 1 < NOC:
-                prep_b(n // NG + 1, "ss")
-            if n >= 2 and (n - 2) % NG == NG - 1:
-                store_out((n - 2) // NG, "ssss")
-            if n >= 1:
-                second(n - 1)
-        second(N_UNITS - 1)
+            m = n - LAG if n >= LAG else None
+            w_banks(n, m)
+            for kind, k in pending:
+                quantise(kind, k)
+            w_quantise(n)
+            if m is not None and m % NG == NG - 1:
+                store_out(m // NG, "ssss")
+            pending = later.get(n, [])
+            for kind, k in pending:
+                group(kind, k, "vs" if kind == "a" else "ss")
+        for m in range(N_UNITS - LAG, N_UNITS):
+            for tt in range(4):
+                second_pass(m, tt)
         store_out(NOC - 1, "svsv")

@@ -46,6 +46,8 @@ def tile_veralayer_pa_kernel(tc, x, A, B, d_A, d_B, out):
         da_b = const.tile([P, 4], BF16, name="da_b")
         da_f = const.tile([P, 4], F32, name="da_f")
         db_bc = [const.tile([P, CH], BF16, name="db_bc%d" % c) for c in range(NOC)]
+        db_row = const.tile([P, DO], BF16, name="db_row")
+        ones = const.tile([P, P], BF16, name="ones")
         a_raw = [raw.tile([P, 4, CH], BF16, name="a_raw%d" % g) for g in range(NG)]
         x_raw = [raw.tile([P, 4 * CH], BF16, name="x_raw%d" % g) for g in range(NG)]
         b_raw = [raw.tile([P, 4 * R], BF16, name="b_raw%d" % c) for c in range(NOC)]
@@ -58,18 +60,19 @@ def tile_veralayer_pa_kernel(tc, x, A, B, d_A, d_B, out):
                 nc.sync.dma_start(
                     out=x_raw[k][:].rearrange("p (tt i) -> p tt i", tt=4), in_=x_v[:, :, k * CH : (k + 1) * CH]
                 )
-            elif kind == "b":
+            else:
                 nc.sync.dma_start(
                     out=b_raw[k][:].rearrange("p (ot r) -> p ot r", ot=4), in_=b_v[:, 4 * k : 4 * k + 4, :]
                 )
-            else:
-                nc.sync.dma_start(out=db_bc[k][:], in_=d_B[k * CH : (k + 1) * CH].partition_broadcast(P))
 
+        nc.vector.memset(db_row[:], 0.0)
+        nc.vector.memset(ones[:], 1.0)
+        nc.sync.dma_start(out=db_row[0:1, :], in_=d_B.rearrange("(a o) -> a o", a=1))
         nc.sync.dma_start(
             out=da_b[:].rearrange("p (u e) -> p u e", u=2), in_=d_A.rearrange("(u p e) -> p u e", u=2, e=2)
         )
         make_identity(nc, ident_f[:])
-        for kind, k in (("a", 0), ("b", 0), ("a", 1), ("d", 0), ("a", 2), ("x", 0), ("a", 3), ("x", 1), ("d", 1), ("b", 1), ("x", 2), ("x", 3), ("d", 2), ("b", 2), ("d", 3), ("b", 3)):
+        for kind, k in (("a", 0), ("b", 0), ("a", 1), ("a", 2), ("x", 0), ("a", 3), ("x", 1), ("b", 1), ("x", 2), ("x", 3), ("b", 2), ("b", 3)):
             load(kind, k)
         nc.vector.tensor_copy(out=da_f[:], in_=da_b[:])
 
@@ -127,6 +130,11 @@ def tile_veralayer_pa_kernel(tc, x, A, B, d_A, d_B, out):
                     gk32[:, half * CH : (half + 1) * CH].rearrange("p (j o u) -> p j o u", j=2, u=2),
                     banks[half][:].rearrange("p j u o -> p j o u"),
                 )
+
+        def spread_db(c, eng):
+            bank = ps_w.tile([P, CH], F32, name="bank_d", tag="w")
+            nc.tensor.matmul(out=bank[:], lhsT=ones[:], rhs=db_row[:, c * CH : (c + 1) * CH], start=True, stop=True)
+            copy_out(eng, db_bc[c][:], bank[:])
 
         def group(kind, k, engs):
             if kind == "a":
@@ -205,6 +213,8 @@ def tile_veralayer_pa_kernel(tc, x, A, B, d_A, d_B, out):
                     nc.scalar.activation(out=o_sb[:], in_=acc[tt][:], func=COPY, scale=SCALE)
                 nc.sync.dma_start(out=out_v[tt * P : (tt + 1) * P, oc * CH : (oc + 1) * CH], in_=o_sb[:])
 
+        for c in range(NOC):
+            spread_db(c, "vsvs"[c])
         group("a", 0, "vs")
         group("b", 0, "vs")
         quantise("a", 0)

@@ -7,6 +7,7 @@ F32 = mybir.dt.float32
 BF16 = mybir.dt.bfloat16
 U32 = mybir.dt.uint32
 U8 = mybir.dt.uint8
+I32 = mybir.dt.int32
 FP8X4 = mybir.dt.float8_e4m3fn_x4
 MULT = mybir.AluOpType.mult
 ADD = mybir.AluOpType.add
@@ -65,7 +66,7 @@ def tile_veralayer_pa_kernel(tc, x, A, B, d_A, d_B, out):
                     out=b_raw[k][:].rearrange("p (ot r) -> p ot r", ot=4), in_=b_v[:, 4 * k : 4 * k + 4, :]
                 )
 
-        nc.vector.memset(db_row[:], 0.0)
+        nc.vector.memset(db_row[:].bitcast(I32), 0)
         nc.vector.memset(ones[:], 1.0)
         nc.sync.dma_start(out=db_row[0:1, :], in_=d_B.rearrange("(a o) -> a o", a=1))
         nc.sync.dma_start(

@@ -7,22 +7,28 @@ F32 = mybir.dt.float32
 BF16 = mybir.dt.bfloat16
 U32 = mybir.dt.uint32
 U8 = mybir.dt.uint8
-I32 = mybir.dt.int32
 FP8X4 = mybir.dt.float8_e4m3fn_x4
 MULT = mybir.AluOpType.mult
 ADD = mybir.AluOpType.add
 COPY = mybir.ActivationFunctionType.Copy
 
 P = 128
-TOK, DI, DO, R = 512, 2048, 2048, 512
-CH = 512
-NG = DI // CH
-NOC = DO // CH
-N_UNITS = NOC * NG
-SCALE = 0.125
+PACK = 4
+CHUNK = P * PACK
+TOKENS, D_IN, D_OUT, RANK = 512, 2048, 2048, 512
+N_G = D_IN // CHUNK
+N_OC = D_OUT // CHUNK
+N_TT = TOKENS // P
+N_OB = CHUNK // P
+N_UNITS = N_OC * N_G
+OUT_SCALE = 0.125
 LAG = 3
-G0 = 0
-FLOPS = 2 * DO * DI * R + 2 * TOK * DI * DO
+AHEAD = 3
+FLOPS = 2 * D_OUT * D_IN * RANK + 2 * TOKENS * D_IN * D_OUT
+
+
+def first_use(kind, k):
+    return {"a": k, "b": N_G * k, "d": N_G * k, "x": k + LAG}[kind]
 
 
 def tile_veralayer_pa_kernel(tc, x, A, B, d_A, d_B, out):
@@ -32,128 +38,142 @@ def tile_veralayer_pa_kernel(tc, x, A, B, d_A, d_B, out):
         const = ctx.enter_context(tc.tile_pool(name="const", bufs=1))
         raw = ctx.enter_context(tc.tile_pool(name="raw", bufs=1))
         keep = ctx.enter_context(tc.tile_pool(name="keep", bufs=1))
-        grp = ctx.enter_context(tc.tile_pool(name="grp", bufs=4))
-        wgp = ctx.enter_context(tc.tile_pool(name="wgp", bufs=2))
-        outp = ctx.enter_context(tc.tile_pool(name="outp", bufs=6))
-        ps_w = ctx.enter_context(tc.psum_pool(name="ps_w", bufs=4))
-        ps_o = ctx.enter_context(tc.psum_pool(name="ps_o", bufs=1))
+        stage = ctx.enter_context(tc.tile_pool(name="stage", bufs=4))
+        w_stage = ctx.enter_context(tc.tile_pool(name="w_stage", bufs=2))
+        out_stage = ctx.enter_context(tc.tile_pool(name="out_stage", bufs=N_TT))
+        bank_pool = ctx.enter_context(tc.psum_pool(name="bank_pool", bufs=4))
+        acc_pool = ctx.enter_context(tc.psum_pool(name="acc_pool", bufs=1))
 
-        x_v = x.rearrange("b s i -> (b s) i").rearrange("(tt p) i -> p tt i", p=P)
-        out_v = out.rearrange("b s o -> (b s) o")
-        a_v = A.rearrange("(u p e) i -> u p e i", u=2, e=2)
-        b_v = B.rearrange("(ot p) r -> p ot r", p=P)
+        x_view = x.rearrange("b s i -> (b s) i").rearrange("(tt p) i -> p tt i", p=P)
+        out_view = out.rearrange("b s o -> (b s) o")
+        a_view = A.rearrange("(u p e) i -> u p e i", u=2, e=2)
+        b_view = B.rearrange("(ot p) r -> p ot r", p=P)
 
-        ident_f = const.tile([P, P], F32, name="ident_f")
-        da_b = const.tile([P, 4], BF16, name="da_b")
-        da_f = const.tile([P, 4], F32, name="da_f")
-        db_bc = [const.tile([P, CH], BF16, name="db_bc%d" % c) for c in range(NOC)]
-        db_row = const.tile([P, DO], BF16, name="db_row")
-        ones = const.tile([P, P], BF16, name="ones")
-        a_raw = [raw.tile([P, 4, CH], BF16, name="a_raw%d" % g) for g in range(NG)]
-        x_raw = [raw.tile([P, 4 * CH], BF16, name="x_raw%d" % g) for g in range(NG)]
-        b_raw = [raw.tile([P, 4 * R], BF16, name="b_raw%d" % c) for c in range(NOC)]
+        identity = const.tile([P, P], F32, name="identity")
+        da_bf16 = const.tile([P, PACK], BF16, name="da_bf16")
+        da = const.tile([P, PACK], F32, name="da")
+        db = [const.tile([P, CHUNK], BF16, name="db%d" % oc) for oc in range(N_OC)]
+        a_raw = [raw.tile([P, PACK, CHUNK], BF16, name="a_raw%d" % g) for g in range(N_G)]
+        x_raw = [raw.tile([P, N_TT * CHUNK], BF16, name="x_raw%d" % g) for g in range(N_G)]
+        b_raw = [raw.tile([P, N_OB * RANK], BF16, name="b_raw%d" % oc) for oc in range(N_OC)]
 
-        def load(kind, k):
-            if kind == "a":
-                for u in range(2):
-                    nc.sync.dma_start(out=a_raw[k][:, 2 * u : 2 * u + 2, :], in_=a_v[u][:, :, k * CH : (k + 1) * CH])
-            elif kind == "x":
-                nc.sync.dma_start(
-                    out=x_raw[k][:].rearrange("p (tt i) -> p tt i", tt=4), in_=x_v[:, :, k * CH : (k + 1) * CH]
-                )
-            else:
-                nc.sync.dma_start(
-                    out=b_raw[k][:].rearrange("p (ot r) -> p ot r", ot=4), in_=b_v[:, 4 * k : 4 * k + 4, :]
-                )
-
-        nc.vector.memset(db_row[:].bitcast(I32), 0)
-        nc.vector.memset(ones[:], 1.0)
-        nc.sync.dma_start(out=db_row[0:1, :], in_=d_B.rearrange("(a o) -> a o", a=1))
-        nc.sync.dma_start(
-            out=da_b[:].rearrange("p (u e) -> p u e", u=2), in_=d_A.rearrange("(u p e) -> p u e", u=2, e=2)
-        )
-        make_identity(nc, ident_f[:])
-        for kind, k in (("a", 0), ("b", 0), ("a", 1), ("a", 2), ("x", 0), ("a", 3), ("x", 1), ("b", 1), ("x", 2), ("x", 3), ("b", 2), ("b", 3)):
-            load(kind, k)
-        nc.vector.tensor_copy(out=da_f[:], in_=da_b[:])
-
-        codes = {}
-        for kind, count in (("a", NG), ("x", NG), ("b", NOC), ("w", N_UNITS)):
+        words_of, scales_of = {}, {}
+        for kind, count in (("a", N_G), ("x", N_G), ("b", N_OC), ("w", N_UNITS)):
             for k in range(count):
-                codes[(kind, k)] = (
-                    keep.tile([P, CH], U32, name="%s_c%d" % (kind, k), align_bytes=64),
-                    keep.tile([P, CH], U8, name="%s_s%d" % (kind, k), align_bytes=64),
-                )
-        grouped = {}
-        acc = {}
+                words_of[(kind, k)] = keep.tile([P, CHUNK], U32, name="%s_words%d" % (kind, k), align_bytes=64)
+                scales_of[(kind, k)] = keep.tile([P, CHUNK], U8, name="%s_scales%d" % (kind, k), align_bytes=64)
 
         def words(kind, k, lo, hi):
-            return codes[(kind, k)][0][:, lo:hi].bitcast(FP8X4)
+            return words_of[(kind, k)][:, lo:hi].bitcast(FP8X4)
 
         def scales(kind, k, lo, hi):
-            return codes[(kind, k)][1][:, lo:hi]
+            return scales_of[(kind, k)][:, lo:hi]
 
-        def copy_out(eng, dst, src):
-            if eng == "v":
+        def load(kind, k):
+            cols = slice(k * CHUNK, (k + 1) * CHUNK)
+            if kind == "a":
+                for u in range(2):
+                    nc.sync.dma_start(out=a_raw[k][:, 2 * u : 2 * u + 2, :], in_=a_view[u][:, :, cols])
+            elif kind == "x":
+                nc.sync.dma_start(out=x_raw[k][:].rearrange("p (tt i) -> p tt i", tt=N_TT), in_=x_view[:, :, cols])
+            elif kind == "b":
+                nc.sync.dma_start(
+                    out=b_raw[k][:].rearrange("p (ot r) -> p ot r", ot=N_OB), in_=b_view[:, N_OB * k : N_OB * (k + 1), :]
+                )
+            else:
+                nc.sync.dma_start(out=db[k][:], in_=d_B[cols].partition_broadcast(P))
+
+        chunks = sorted(
+            [
+                (first_use(kind, k), "xabd".index(kind), kind, k)
+                for kind, count in (("x", N_G), ("a", N_G), ("b", N_OC), ("d", N_OC))
+                for k in range(count)
+            ]
+        )
+        nc.sync.dma_start(
+            out=da_bf16[:].rearrange("p (u e) -> p u e", u=2), in_=d_A.rearrange("(u p e) -> p u e", u=2, e=2)
+        )
+        make_identity(nc, identity[:])
+        for use, rank, kind, k in chunks:
+            load(kind, k)
+        nc.vector.tensor_copy(out=da[:], in_=da_bf16[:])
+
+        grouped = {}
+
+        def copy(on_vector, dst, src):
+            if on_vector:
                 nc.vector.tensor_copy(out=dst, in_=src)
             else:
                 nc.scalar.copy(out=dst, in_=src)
 
-        def group_a(g, engs):
-            a_sc = grp.tile([P, 4, CH], BF16, name="a_sc", tag="a_sc")
-            for t in range(4):
+        def group_a(g):
+            scaled = stage.tile([P, PACK, CHUNK], BF16, name="scaled", tag="scaled")
+            for t in range(PACK):
                 nc.vector.tensor_scalar(
-                    out=a_sc[:, t, :], in0=a_raw[g][:, t, :], scalar1=da_f[:, t : t + 1], scalar2=0.0, op0=MULT, op1=ADD
+                    out=scaled[:, t, :], in0=a_raw[g][:, t, :], scalar1=da[:, t : t + 1], scalar2=0.0, op0=MULT, op1=ADD
                 )
-            ga = grp.tile([P, 4 * CH], BF16, name="ga", tag="grp", align_bytes=64)
-            grouped[("a", g)] = ga
+            tile = stage.tile([P, PACK * CHUNK], BF16, name="grouped_a", tag="grouped", align_bytes=64)
+            grouped[("a", g)] = tile
             for u in range(2):
-                copy_out(
-                    engs[u],
-                    ga[:, 2 * u * CH : 2 * (u + 1) * CH].rearrange("p (e c t) -> p e c t", e=2, t=4),
-                    a_sc[:].rearrange("p t (u c e) -> p u e c t", u=2, e=2)[:, u],
+                copy(
+                    u == 0,
+                    tile[:, 2 * u * CHUNK : 2 * (u + 1) * CHUNK].rearrange("p (e c t) -> p e c t", e=2, t=PACK),
+                    scaled[:].rearrange("p t (u c e) -> p u e c t", u=2, e=2)[:, u],
                 )
 
-        def group_t(kind, k, engs):
-            src32 = (x_raw[k] if kind == "x" else b_raw[k])[:].bitcast(F32)
-            gk = grp.tile([P, 4 * CH], BF16, name="gk", tag="grp", align_bytes=64)
-            grouped[(kind, k)] = gk
-            gk32 = gk[:].bitcast(F32)
-            banks = [ps_w.tile([P, 2, 2, P], F32, name="bank_t", tag="w") for half in range(2)]
+        def group_transposed(kind, k, vector_helps):
+            source = (x_raw[k] if kind == "x" else b_raw[k])[:].bitcast(F32)
+            tile = stage.tile([P, PACK * CHUNK], BF16, name="grouped_t", tag="grouped", align_bytes=64)
+            grouped[(kind, k)] = tile
+            tile_words = tile[:].bitcast(F32)
+            banks = [bank_pool.tile([P, 2, 2, P], F32, name="bank_t", tag="bank") for half in range(2)]
             for half in range(2):
                 for j in range(2):
                     for u in range(2):
-                        w0 = (2 * half + j) * 256 + u * P
-                        nc.tensor.transpose(banks[half][:, j, u, :], src32[:, w0 : w0 + P], ident_f[:])
+                        first = (2 * half + j) * 2 * P + u * P
+                        nc.tensor.transpose(banks[half][:, j, u, :], source[:, first : first + P], identity[:])
             for half in range(2):
-                copy_out(
-                    engs[half],
-                    gk32[:, half * CH : (half + 1) * CH].rearrange("p (j o u) -> p j o u", j=2, u=2),
-                    banks[half][:].rearrange("p j u o -> p j o u"),
+                copy(
+                    vector_helps and half == 0,
+                    tile_words[:, half * CHUNK : (half + 1) * CHUNK].rearrange("p (j c u) -> p j c u", j=2, u=2),
+                    banks[half][:].rearrange("p j u c -> p j c u"),
                 )
 
-        def spread_db(c, eng):
-            bank = ps_w.tile([P, CH], F32, name="bank_d", tag="w")
-            nc.tensor.matmul(out=bank[:], lhsT=ones[:], rhs=db_row[:, c * CH : (c + 1) * CH], start=True, stop=True)
-            copy_out(eng, db_bc[c][:], bank[:])
-
-        def group(kind, k, engs):
+        def group(kind, k, vector_helps):
             if kind == "a":
-                group_a(k, engs)
+                group_a(k)
             else:
-                group_t(kind, k, engs)
+                group_transposed(kind, k, vector_helps)
 
         def quantise(kind, k):
-            nc.vector.quantize_mx(out=words(kind, k, 0, CH), scales=scales(kind, k, 0, CH), in_=grouped[(kind, k)][:])
+            nc.vector.quantize_mx(out=words(kind, k, 0, CHUNK), scales=scales(kind, k, 0, CHUNK), in_=grouped[(kind, k)][:])
 
-        def w_banks(n, m):
-            oc, g = n // NG, n % NG
-            wgv = wgp.tile([P, 4 * CH], BF16, name="wgv", tag="wgv", align_bytes=64)
-            wgg = wgp.tile([P, CH], BF16, name="wgg", tag="wgg", bufs=1, align_bytes=64) if n >= G0 else None
-            grouped[("w", n)] = (wgv, wgg)
-            for ob in range(4):
-                bank = ps_w.tile([P, 4, P], F32, name="bank_w", tag="w")
-                for t in range(4):
+        def to_prepare(unit):
+            return [(kind, k) for use, rank, kind, k in chunks if use == unit and kind != "d"]
+
+        acc = {}
+
+        def second_matmul_pass(n, tt):
+            oc, g = n // N_G, n % N_G
+            if g == 0:
+                acc[tt] = acc_pool.tile([P, CHUNK], F32, name="acc%d" % tt, tag="acc%d" % tt)
+            nc.tensor.matmul_mx(
+                out=acc[tt][:],
+                lhsT=words("x", g, tt * P, (tt + 1) * P),
+                lhsT_scale=scales("x", g, tt * P, (tt + 1) * P),
+                rhs=words("w", n, 0, CHUNK),
+                rhs_scale=scales("w", n, 0, CHUNK),
+                start=(g == 0),
+                stop=(g == N_G - 1),
+            )
+
+        def first_matmul(n):
+            oc, g = n // N_G, n % N_G
+            by_vector = w_stage.tile([P, 3 * CHUNK], BF16, name="w_by_vector", tag="w_by_vector", align_bytes=64)
+            by_gpsimd = w_stage.tile([P, CHUNK], BF16, name="w_by_gpsimd", tag="w_by_gpsimd", bufs=1, align_bytes=64)
+            for ob in range(N_OB):
+                bank = bank_pool.tile([P, PACK, P], F32, name="bank_w", tag="bank")
+                for t in range(PACK):
                     nc.tensor.matmul_mx(
                         out=bank[:, t, :],
                         lhsT=words("a", g, t * P, (t + 1) * P),
@@ -163,79 +183,63 @@ def tile_veralayer_pa_kernel(tc, x, A, B, d_A, d_B, out):
                         start=True,
                         stop=True,
                     )
-                if m is not None:
-                    second_pass(m, ob)
-                db = db_bc[oc][:, ob * P : (ob + 1) * P].unsqueeze(2).to_broadcast([P, P, 4])
-                if ob == 0 and n >= G0:
-                    wf = wgp.tile([P, CH], F32, name="wf", tag="wf")
-                    nc.scalar.copy(out=wf[:].rearrange("p (o t) -> p o t", t=4), in_=bank[:].rearrange("p t o -> p o t"))
+                if n >= LAG:
+                    second_matmul_pass(n - LAG, ob)
+                bank_ot = bank[:].rearrange("p t o -> p o t")
+                db_ot = db[oc][:, ob * P : (ob + 1) * P].unsqueeze(2).to_broadcast([P, P, PACK])
+                if ob == 0:
+                    in_f32 = w_stage.tile([P, CHUNK], F32, name="w_in_f32", tag="w_in_f32")
+                    nc.scalar.copy(out=in_f32[:].rearrange("p (o t) -> p o t", t=PACK), in_=bank_ot)
                     nc.gpsimd.tensor_tensor(
-                        out=wgg[:].rearrange("p (o t) -> p o t", t=4),
-                        in0=wf[:].rearrange("p (o t) -> p o t", t=4),
-                        in1=db,
+                        out=by_gpsimd[:].rearrange("p (o t) -> p o t", t=PACK),
+                        in0=in_f32[:].rearrange("p (o t) -> p o t", t=PACK),
+                        in1=db_ot,
                         op=MULT,
                     )
                 else:
                     nc.vector.tensor_tensor(
-                        out=wgv[:, ob * CH : (ob + 1) * CH].rearrange("p (o t) -> p o t", t=4),
-                        in0=bank[:].rearrange("p t o -> p o t"),
-                        in1=db,
+                        out=by_vector[:, (ob - 1) * CHUNK : ob * CHUNK].rearrange("p (o t) -> p o t", t=PACK),
+                        in0=bank_ot,
+                        in1=db_ot,
                         op=MULT,
                     )
+            return by_vector, by_gpsimd
 
-        def w_quantise(n):
-            wgv, wgg = grouped[("w", n)]
-            if n < G0:
-                nc.vector.quantize_mx(out=words("w", n, 0, CH), scales=scales("w", n, 0, CH), in_=wgv[:])
-                return
-            for lo, hi, src in ((P, 3 * P, wgv[:, CH : 3 * CH]), (3 * P, 4 * P, wgv[:, 3 * CH : 4 * CH]), (0, P, wgg[:])):
-                nc.vector.quantize_mx(out=words("w", n, lo, hi), scales=scales("w", n, lo, hi), in_=src)
+        def quantise_w(n, by_vector, by_gpsimd):
+            for lo, hi, values in (
+                (P, 3 * P, by_vector[:, 0 : 2 * CHUNK]),
+                (3 * P, 4 * P, by_vector[:, 2 * CHUNK : 3 * CHUNK]),
+                (0, P, by_gpsimd[:]),
+            ):
+                nc.vector.quantize_mx(out=words("w", n, lo, hi), scales=scales("w", n, lo, hi), in_=values)
 
-        def second_pass(n, tt):
-            oc, g = n // NG, n % NG
-            if g == 0:
-                acc[tt] = ps_o.tile([P, CH], F32, name="acc%d" % tt, tag="acc%d" % tt)
-            nc.tensor.matmul_mx(
-                out=acc[tt][:],
-                lhsT=words("x", g, tt * P, (tt + 1) * P),
-                lhsT_scale=scales("x", g, tt * P, (tt + 1) * P),
-                rhs=words("w", n, 0, CH),
-                rhs_scale=scales("w", n, 0, CH),
-                start=(g == 0),
-                stop=(g == NG - 1),
-            )
-
-        def store_out(oc, engs):
-            for tt in range(4):
-                o_sb = outp.tile([P, CH], F32, name="o_sb", tag="o_sb")
-                if engs[tt] == "v":
-                    nc.vector.tensor_scalar_mul(out=o_sb[:], in0=acc[tt][:], scalar1=SCALE)
+        def store_out(oc, vector_helps):
+            for tt in range(N_TT):
+                result = out_stage.tile([P, CHUNK], F32, name="result", tag="result")
+                if vector_helps and tt % 2 == 1:
+                    nc.vector.tensor_scalar_mul(out=result[:], in0=acc[tt][:], scalar1=OUT_SCALE)
                 else:
-                    nc.scalar.activation(out=o_sb[:], in_=acc[tt][:], func=COPY, scale=SCALE)
-                nc.sync.dma_start(out=out_v[tt * P : (tt + 1) * P, oc * CH : (oc + 1) * CH], in_=o_sb[:])
+                    nc.scalar.activation(out=result[:], in_=acc[tt][:], func=COPY, scale=OUT_SCALE)
+                nc.sync.dma_start(out=out_view[tt * P : (tt + 1) * P, oc * CHUNK : (oc + 1) * CHUNK], in_=result[:])
 
-        for c in range(NOC):
-            spread_db(c, "vsvs"[c])
-        group("a", 0, "vs")
-        group("b", 0, "vs")
-        quantise("a", 0)
-        quantise("b", 0)
-        pending = [("a", 1), ("a", 2)]
-        for kind, k in pending:
-            group(kind, k, "vs" if kind == "a" else "ss")
-        later = {0: [("x", 0), ("a", 3)], 1: [("x", 1), ("b", 1)], 2: [("x", 2)], 3: [("x", 3)], 5: [("b", 2)], 9: [("b", 3)]}
+        for kind, k in to_prepare(0):
+            group(kind, k, True)
+        for kind, k in to_prepare(0):
+            quantise(kind, k)
+        waiting = [chunk for unit in range(1, AHEAD) for chunk in to_prepare(unit)]
+        for kind, k in waiting:
+            group(kind, k, False)
         for n in range(N_UNITS):
-            m = n - LAG if n >= LAG else None
-            w_banks(n, m)
-            for kind, k in pending:
+            by_vector, by_gpsimd = first_matmul(n)
+            for kind, k in waiting:
                 quantise(kind, k)
-            w_quantise(n)
-            if m is not None and m % NG == NG - 1:
-                store_out(m // NG, "ssss")
-            pending = later.get(n, [])
-            for kind, k in pending:
-                group(kind, k, "vs" if kind == "a" else "ss")
-        for m in range(N_UNITS - LAG, N_UNITS):
-            for tt in range(4):
-                second_pass(m, tt)
-        store_out(NOC - 1, "svsv")
+            quantise_w(n, by_vector, by_gpsimd)
+            if n >= LAG and (n - LAG) % N_G == N_G - 1:
+                store_out((n - LAG) // N_G, False)
+            waiting = to_prepare(n + AHEAD)
+            for kind, k in waiting:
+                group(kind, k, False)
+        for n in range(N_UNITS - LAG, N_UNITS):
+            for tt in range(N_TT):
+                second_matmul_pass(n, tt)
+        store_out(N_OC - 1, True)

from contextlib import ExitStack

import concourse.mybir as mybir
from concourse.masks import make_identity

F32 = mybir.dt.float32
BF16 = mybir.dt.bfloat16
U32 = mybir.dt.uint32
U8 = mybir.dt.uint8
FP8X4 = mybir.dt.float8_e4m3fn_x4
MULT = mybir.AluOpType.mult
ADD = mybir.AluOpType.add
COPY = mybir.ActivationFunctionType.Copy

P = 128
PACK = 4
CHUNK = P * PACK
TOKENS, D_IN, D_OUT, RANK = 512, 2048, 2048, 512
N_G = D_IN // CHUNK
N_OC = D_OUT // CHUNK
N_TT = TOKENS // P
N_OB = CHUNK // P
N_UNITS = N_OC * N_G
OUT_SCALE = 0.125
LAG = 3
AHEAD = 3
FLOPS = 2 * D_OUT * D_IN * RANK + 2 * TOKENS * D_IN * D_OUT


def first_use(kind, k):
    return {"a": k, "b": N_G * k, "d": N_G * k, "x": k + LAG}[kind]


def tile_veralayer_pa_kernel(tc, x, A, B, d_A, d_B, out):
    nc = tc.nc
    with ExitStack() as ctx:
        ctx.enter_context(tc.manual_schedule())
        const = ctx.enter_context(tc.tile_pool(name="const", bufs=1))
        raw = ctx.enter_context(tc.tile_pool(name="raw", bufs=1))
        keep = ctx.enter_context(tc.tile_pool(name="keep", bufs=1))
        stage = ctx.enter_context(tc.tile_pool(name="stage", bufs=4))
        w_stage = ctx.enter_context(tc.tile_pool(name="w_stage", bufs=2))
        out_stage = ctx.enter_context(tc.tile_pool(name="out_stage", bufs=N_TT))
        bank_pool = ctx.enter_context(tc.psum_pool(name="bank_pool", bufs=4))
        acc_pool = ctx.enter_context(tc.psum_pool(name="acc_pool", bufs=1))

        x_view = x.rearrange("b s i -> (b s) i").rearrange("(tt p) i -> p tt i", p=P)
        out_view = out.rearrange("b s o -> (b s) o")
        a_view = A.rearrange("(u p e) i -> u p e i", u=2, e=2)
        b_view = B.rearrange("(ot p) r -> p ot r", p=P)

        identity = const.tile([P, P], F32, name="identity")
        da_bf16 = const.tile([P, PACK], BF16, name="da_bf16")
        da = const.tile([P, PACK], F32, name="da")
        db = [const.tile([P, CHUNK], BF16, name="db%d" % oc) for oc in range(N_OC)]
        a_raw = [raw.tile([P, PACK, CHUNK], BF16, name="a_raw%d" % g) for g in range(N_G)]
        x_raw = [raw.tile([P, N_TT * CHUNK], BF16, name="x_raw%d" % g) for g in range(N_G)]
        b_raw = [raw.tile([P, N_OB * RANK], BF16, name="b_raw%d" % oc) for oc in range(N_OC)]

        words_of, scales_of = {}, {}
        for kind, count in (("a", N_G), ("x", N_G), ("b", N_OC), ("w", N_UNITS)):
            for k in range(count):
                words_of[(kind, k)] = keep.tile([P, CHUNK], U32, name="%s_words%d" % (kind, k), align_bytes=64)
                scales_of[(kind, k)] = keep.tile([P, CHUNK], U8, name="%s_scales%d" % (kind, k), align_bytes=64)

        def words(kind, k, lo, hi):
            return words_of[(kind, k)][:, lo:hi].bitcast(FP8X4)

        def scales(kind, k, lo, hi):
            return scales_of[(kind, k)][:, lo:hi]

        def load(kind, k):
            cols = slice(k * CHUNK, (k + 1) * CHUNK)
            if kind == "a":
                for u in range(2):
                    nc.sync.dma_start(out=a_raw[k][:, 2 * u : 2 * u + 2, :], in_=a_view[u][:, :, cols])
            elif kind == "x":
                nc.sync.dma_start(out=x_raw[k][:].rearrange("p (tt i) -> p tt i", tt=N_TT), in_=x_view[:, :, cols])
            elif kind == "b":
                nc.sync.dma_start(
                    out=b_raw[k][:].rearrange("p (ot r) -> p ot r", ot=N_OB), in_=b_view[:, N_OB * k : N_OB * (k + 1), :]
                )
            else:
                nc.sync.dma_start(out=db[k][:], in_=d_B[cols].partition_broadcast(P))

        chunks = sorted(
            [
                (first_use(kind, k), "xabd".index(kind), kind, k)
                for kind, count in (("x", N_G), ("a", N_G), ("b", N_OC), ("d", N_OC))
                for k in range(count)
            ]
        )
        nc.sync.dma_start(
            out=da_bf16[:].rearrange("p (u e) -> p u e", u=2), in_=d_A.rearrange("(u p e) -> p u e", u=2, e=2)
        )
        make_identity(nc, identity[:])
        for use, rank, kind, k in chunks:
            load(kind, k)
        nc.vector.tensor_copy(out=da[:], in_=da_bf16[:])

        grouped = {}

        def copy(on_vector, dst, src):
            if on_vector:
                nc.vector.tensor_copy(out=dst, in_=src)
            else:
                nc.scalar.copy(out=dst, in_=src)

        def group_a(g):
            scaled = stage.tile([P, PACK, CHUNK], BF16, name="scaled", tag="scaled")
            for t in range(PACK):
                nc.vector.tensor_scalar(
                    out=scaled[:, t, :], in0=a_raw[g][:, t, :], scalar1=da[:, t : t + 1], scalar2=0.0, op0=MULT, op1=ADD
                )
            tile = stage.tile([P, PACK * CHUNK], BF16, name="grouped_a", tag="grouped", align_bytes=64)
            grouped[("a", g)] = tile
            for u in range(2):
                copy(
                    u == 0,
                    tile[:, 2 * u * CHUNK : 2 * (u + 1) * CHUNK].rearrange("p (e c t) -> p e c t", e=2, t=PACK),
                    scaled[:].rearrange("p t (u c e) -> p u e c t", u=2, e=2)[:, u],
                )

        def group_transposed(kind, k, vector_helps):
            source = (x_raw[k] if kind == "x" else b_raw[k])[:].bitcast(F32)
            tile = stage.tile([P, PACK * CHUNK], BF16, name="grouped_t", tag="grouped", align_bytes=64)
            grouped[(kind, k)] = tile
            tile_words = tile[:].bitcast(F32)
            banks = [bank_pool.tile([P, 2, 2, P], F32, name="bank_t", tag="bank") for half in range(2)]
            for half in range(2):
                for j in range(2):
                    for u in range(2):
                        first = (2 * half + j) * 2 * P + u * P
                        nc.tensor.transpose(banks[half][:, j, u, :], source[:, first : first + P], identity[:])
            for half in range(2):
                copy(
                    vector_helps and half == 0,
                    tile_words[:, half * CHUNK : (half + 1) * CHUNK].rearrange("p (j c u) -> p j c u", j=2, u=2),
                    banks[half][:].rearrange("p j u c -> p j c u"),
                )

        def group(kind, k, vector_helps):
            if kind == "a":
                group_a(k)
            else:
                group_transposed(kind, k, vector_helps)

        def quantise(kind, k):
            nc.vector.quantize_mx(out=words(kind, k, 0, CHUNK), scales=scales(kind, k, 0, CHUNK), in_=grouped[(kind, k)][:])

        def to_prepare(unit):
            return [(kind, k) for use, rank, kind, k in chunks if use == unit and kind != "d"]

        acc = {}

        def second_matmul_pass(n, tt):
            oc, g = n // N_G, n % N_G
            if g == 0:
                acc[tt] = acc_pool.tile([P, CHUNK], F32, name="acc%d" % tt, tag="acc%d" % tt)
            nc.tensor.matmul_mx(
                out=acc[tt][:],
                lhsT=words("x", g, tt * P, (tt + 1) * P),
                lhsT_scale=scales("x", g, tt * P, (tt + 1) * P),
                rhs=words("w", n, 0, CHUNK),
                rhs_scale=scales("w", n, 0, CHUNK),
                start=(g == 0),
                stop=(g == N_G - 1),
            )

        def first_matmul(n):
            oc, g = n // N_G, n % N_G
            by_vector = w_stage.tile([P, 3 * CHUNK], BF16, name="w_by_vector", tag="w_by_vector", align_bytes=64)
            by_gpsimd = w_stage.tile([P, CHUNK], BF16, name="w_by_gpsimd", tag="w_by_gpsimd", bufs=1, align_bytes=64)
            for ob in range(N_OB):
                bank = bank_pool.tile([P, PACK, P], F32, name="bank_w", tag="bank")
                for t in range(PACK):
                    nc.tensor.matmul_mx(
                        out=bank[:, t, :],
                        lhsT=words("a", g, t * P, (t + 1) * P),
                        lhsT_scale=scales("a", g, t * P, (t + 1) * P),
                        rhs=words("b", oc, ob * P, (ob + 1) * P),
                        rhs_scale=scales("b", oc, ob * P, (ob + 1) * P),
                        start=True,
                        stop=True,
                    )
                if n >= LAG:
                    second_matmul_pass(n - LAG, ob)
                bank_ot = bank[:].rearrange("p t o -> p o t")
                db_ot = db[oc][:, ob * P : (ob + 1) * P].unsqueeze(2).to_broadcast([P, P, PACK])
                if ob == 0:
                    in_f32 = w_stage.tile([P, CHUNK], F32, name="w_in_f32", tag="w_in_f32")
                    nc.scalar.copy(out=in_f32[:].rearrange("p (o t) -> p o t", t=PACK), in_=bank_ot)
                    nc.gpsimd.tensor_tensor(
                        out=by_gpsimd[:].rearrange("p (o t) -> p o t", t=PACK),
                        in0=in_f32[:].rearrange("p (o t) -> p o t", t=PACK),
                        in1=db_ot,
                        op=MULT,
                    )
                else:
                    nc.vector.tensor_tensor(
                        out=by_vector[:, (ob - 1) * CHUNK : ob * CHUNK].rearrange("p (o t) -> p o t", t=PACK),
                        in0=bank_ot,
                        in1=db_ot,
                        op=MULT,
                    )
            return by_vector, by_gpsimd

        def quantise_w(n, by_vector, by_gpsimd):
            for lo, hi, values in (
                (P, 3 * P, by_vector[:, 0 : 2 * CHUNK]),
                (3 * P, 4 * P, by_vector[:, 2 * CHUNK : 3 * CHUNK]),
                (0, P, by_gpsimd[:]),
            ):
                nc.vector.quantize_mx(out=words("w", n, lo, hi), scales=scales("w", n, lo, hi), in_=values)

        def store_out(oc, vector_helps):
            for tt in range(N_TT):
                result = out_stage.tile([P, CHUNK], F32, name="result", tag="result")
                if vector_helps and tt % 2 == 1:
                    nc.vector.tensor_scalar_mul(out=result[:], in0=acc[tt][:], scalar1=OUT_SCALE)
                else:
                    nc.scalar.activation(out=result[:], in_=acc[tt][:], func=COPY, scale=OUT_SCALE)
                nc.sync.dma_start(out=out_view[tt * P : (tt + 1) * P, oc * CHUNK : (oc + 1) * CHUNK], in_=result[:])

        for kind, k in to_prepare(0):
            group(kind, k, True)
        for kind, k in to_prepare(0):
            quantise(kind, k)
        waiting = [chunk for unit in range(1, AHEAD) for chunk in to_prepare(unit)]
        for kind, k in waiting:
            group(kind, k, False)
        for n in range(N_UNITS):
            by_vector, by_gpsimd = first_matmul(n)
            for kind, k in waiting:
                quantise(kind, k)
            quantise_w(n, by_vector, by_gpsimd)
            if n >= LAG and (n - LAG) % N_G == N_G - 1:
                store_out((n - LAG) // N_G, False)
            waiting = to_prepare(n + AHEAD)
            for kind, k in waiting:
                group(kind, k, False)
        for n in range(N_UNITS - LAG, N_UNITS):
            for tt in range(N_TT):
                second_matmul_pass(n, tt)
        store_out(N_OC - 1, True)
